import numpy as np
import ml_dtypes


def mxq(x, axis, fmt="e4m3"):
    dtype, down = {"e4m3": (ml_dtypes.float8_e4m3fn, 7), "e5m2": (ml_dtypes.float8_e5m2, 14)}[fmt]
    v = np.moveaxis(np.asarray(x, np.float32).astype(ml_dtypes.bfloat16).astype(np.float64), axis, -1)
    blocks = v.reshape(v.shape[:-1] + (-1, 32))
    amax = np.abs(blocks).max(-1, keepdims=True)
    byte = np.maximum(np.where(amax > 0, np.frexp(amax)[1] - 1 + 127, 0) - down, 1)
    scale = np.exp2(byte - 127.0)
    codes = (blocks / scale).astype(np.float32).astype(dtype).astype(np.float64)
    return np.moveaxis((codes * scale).reshape(v.shape), -1, axis)


WIDE = False


def mx_kscale(k):
    if not WIDE:
        return np.ones(k)
    levels = np.array([10, -10, 5, -5, 0])
    a = np.random.permutation(np.resize(levels, k // 512 * 4)).reshape(k // 512, 4)
    idx = np.arange(k)
    return np.exp2(a[idx // 512, idx % 128 // 32])


BF16 = ml_dtypes.bfloat16


def bf(x):
    return np.asarray(x, np.float32).astype(BF16)


def f64(x):
    return np.asarray(x).astype(np.float64)


B, T, C, CO, HS, DW, DA, DV, DG = 4, 128, 2048, 2048, 64, 128, 128, 128, 256
H = CO // HS
EPS_NORM = 1e-12


def sigmoid(u):
    return 1.0 / (1.0 + np.exp(-u))


def setup_inputs():
    n = np.random.standard_normal
    s = mx_kscale(C)
    return {
        "x": bf(n((B, T, C)) * s),
        "x_k": bf(n((1, 1, C)) * 0.3),
        "W_k": bf(n((CO, C)) / np.sqrt(C) / s),
        "a_hid": bf(n((B, T, DA))),
        "a2": bf(n((DA, CO)) / np.sqrt(DA)),
        "a0": bf(n((1, 1, CO)) * 0.5),
        "k_k": bf(0.71 + n((1, 1, CO)) * 0.2),
        "k_a": bf(1.02 + n((1, 1, CO)) * 0.2),
    }


def reference(x, x_k, W_k, a_hid, a2, a0, k_k, k_a):
    x = f64(x)
    prev = np.concatenate([np.zeros_like(x[:, :1]), x[:, :-1]], axis=1)
    xk = x + (prev - x) * f64(x_k)
    k = mxq(xk, 2, "e4m3") @ mxq(f64(W_k), 1, "e4m3").T
    a = sigmoid(f64(a0) + f64(a_hid) @ f64(a2))
    kkh = (k * f64(k_k)).reshape(B, T, H, HS)
    nrm = np.sqrt(np.sum(kkh * kkh, axis=-1, keepdims=True))
    kk = (kkh / np.maximum(nrm, EPS_NORM)).reshape(B, T, CO)
    k_out = k * (1.0 + (a - 1.0) * f64(k_a))
    return k_out, kk

@@ -1,0 +1,278 @@
+from contextlib import ExitStack
+
+import concourse.mybir as mybir
+from concourse.masks import make_identity
+
+BF16 = mybir.dt.bfloat16
+F32 = mybir.dt.float32
+U32 = mybir.dt.uint32
+U8 = mybir.dt.uint8
+FP8X4 = mybir.dt.float8_e4m3fn_x4
+ACT = mybir.ActivationFunctionType
+ALU = mybir.AluOpType
+
+P = 128
+SEQS = 4
+T = 128
+TOKENS = SEQS * T
+C = 2048
+CO = 2048
+DA = 128
+HEAD = 64
+PACK = 4
+K_PASS = P * PACK
+PASSES = C // K_PASS
+HALF = K_PASS // 2
+N_TILE = 512
+N_TILES = CO // N_TILE
+BLOCKS = N_TILE // P
+HEADS = N_TILE // HEAD
+BANK_WORDS = 512
+BANKS = 8
+UNITS = N_TILES * PASSES
+AHEAD = 1
+NORM_FLOOR = 1e-12
+
+FLOPS = 2 * TOKENS * C * CO + 2 * TOKENS * DA * CO
+
+
+def tile_full_tmix_params_pa_kernel(tc, x, x_k, W_k, a_hid, a2, a0, k_k, k_a, out_0, out_1):
+    nc = tc.nc
+    with ExitStack() as ctx:
+        ctx.enter_context(tc.manual_schedule())
+        keep = ctx.enter_context(tc.tile_pool(name="keep", bufs=1))
+        x_pool = ctx.enter_context(tc.tile_pool(name="x_pool", bufs=PASSES))
+        w_pool = ctx.enter_context(tc.tile_pool(name="w_pool", bufs=CO // P))
+        stage = ctx.enter_context(tc.tile_pool(name="stage", bufs=2))
+        wq_pool = ctx.enter_context(tc.tile_pool(name="wq_pool", bufs=2 * PASSES + AHEAD))
+        gate_t_pool = ctx.enter_context(tc.tile_pool(name="gate_t_pool", bufs=CO // P))
+        gate_pool = ctx.enter_context(tc.tile_pool(name="gate_pool", bufs=SEQS + 2))
+        tail = ctx.enter_context(tc.tile_pool(name="tail", bufs=3))
+
+        ident_bf = keep.tile([P, P], BF16)
+        make_identity(nc, ident_bf[:])
+        ident_f32 = keep.tile([P, P], F32)
+        make_identity(nc, ident_f32[:])
+
+        mix_rows = keep.tile([P, HALF], BF16)
+        nc.vector.memset(mix_rows[:], 0.0)
+        gate_rows = keep.tile([P, P], BF16)
+        nc.vector.memset(gate_rows[:], 0.0)
+        hid = keep.tile([P, SEQS, DA], BF16)
+        a2_sb = keep.tile([DA, CO], BF16)
+        k_k_all = keep.tile([P, CO], BF16)
+
+        nc.sync.dma_start(out=mix_rows[0 : C // HALF, :], in_=x_k.rearrange("a b (r c) -> (a b r) c", c=HALF))
+        x_tiles = []
+        for g in range(PASSES):
+            x_g = x_pool.tile([P, SEQS, K_PASS], BF16, name="x_g")
+            nc.sync.dma_start(out=x_g[:], in_=x[:, :, g * K_PASS : (g + 1) * K_PASS].rearrange("b t c -> t b c"))
+            x_tiles.append(x_g)
+            if g == 0:
+                nc.sync.dma_start(out=hid[:], in_=a_hid.rearrange("b t d -> t b d"))
+                nc.sync.dma_start(out=a2_sb[:], in_=a2)
+                nc.sync.dma_start(out=gate_rows[0 : CO // P, :], in_=a0.rearrange("a b (j p) -> (a b j) p", p=P))
+                nc.sync.dma_start(
+                    out=gate_rows[CO // P : 2 * CO // P, :], in_=k_a.rearrange("a b (j p) -> (a b j) p", p=P)
+                )
+        w_tiles = []
+        for i in range(CO // P):
+            w_i = w_pool.tile([P, C], BF16, name="w_i")
+            nc.sync.dma_start(out=w_i[:], in_=W_k[i * P : (i + 1) * P, :])
+            w_tiles.append(w_i)
+            if i == BLOCKS - 1:
+                nc.sync.dma_start(out=k_k_all[:], in_=k_k.rearrange("a b c -> (a b c)").partition_broadcast(P))
+
+        mix = keep.tile([P, 2, C // HALF], F32)
+        stay = keep.tile([P, 2, C // HALF], F32)
+        neg = keep.tile([P, 2 * CO // P], F32)
+        hid_t = keep.tile([DA, TOKENS], BF16)
+        xk_codes = keep.tile([P, PASSES, TOKENS], U32, align_bytes=64)
+        xk_scales = keep.tile([P, PASSES, TOKENS], U8, align_bytes=64)
+        shifted_ring = [keep.tile([P, SEQS, T], F32, name="shifted%d" % i) for i in range(3)]
+        for shifted in shifted_ring:
+            nc.vector.memset(shifted[:, :, 0:1], 0.0)
+
+        def mix_channels(banks, g, t, planes):
+            u, e = divmod(t, 2)
+            r = 2 * g + u
+            x_t = banks.tile([P, TOKENS], BF16, tag="bank")
+            for b in range(SEQS):
+                nc.tensor.transpose(
+                    x_t[:, b * T : (b + 1) * T], x_tiles[g][:, b, u * HALF + e : (u + 1) * HALF : 2], ident_bf[:]
+                )
+            shifted = shifted_ring[(g * PACK + t) % len(shifted_ring)]
+            nc.scalar.activation(
+                out=shifted[:, :, 1:T],
+                in_=x_t[:].rearrange("p (b r) -> p b r", b=SEQS)[:, :, 0 : T - 1],
+                func=ACT.Copy,
+                scale=mix[:, e, r : r + 1],
+            )
+            nc.vector.scalar_tensor_tensor(
+                out=planes[:, t, :],
+                in0=x_t[:],
+                scalar=stay[:, e, r : r + 1],
+                in1=shifted[:].rearrange("p b r -> p (b r)"),
+                op0=ALU.mult,
+                op1=ALU.add,
+            )
+
+        def quantise_tokens(g, planes):
+            grouped = stage.tile([P, TOKENS * PACK], BF16, align_bytes=64)
+            nc.vector.tensor_copy(
+                out=grouped[:].rearrange("p (c i t) -> p c t i", i=4, t=PACK),
+                in_=planes[:].rearrange("p t (c i) -> p c t i", i=4),
+            )
+            nc.vector.quantize_mx(out=xk_codes[:, g, :].bitcast(FP8X4), scales=xk_scales[:, g, :], in_=grouped[:])
+
+        def regroup_weights(banks, unit):
+            n, g = divmod(unit, PASSES)
+            w_grouped = stage.tile([P, N_TILE * PACK], BF16, align_bytes=64, bufs=3)
+            words = w_grouped[:].bitcast(F32)
+            for h in range(BLOCKS // 2):
+                w_t = banks.tile([P, 2, 2 * P], F32, tag="bank")
+                for u in range(2):
+                    for i in range(2):
+                        first = (g * K_PASS + u * HALF) // 2
+                        nc.tensor.transpose(
+                            w_t[:, u, i * P : (i + 1) * P],
+                            w_tiles[n * BLOCKS + 2 * h + i][:].bitcast(F32)[:, first : first + P],
+                            ident_f32[:],
+                        )
+                nc.scalar.copy(
+                    out=words[:, h * BANK_WORDS : (h + 1) * BANK_WORDS].rearrange("p (c u) -> p c u", u=2),
+                    in_=w_t[:].rearrange("p u c -> p c u"),
+                )
+            return w_grouped
+
+        def quantise_weights(w_grouped):
+            w_codes = wq_pool.tile([P, N_TILE], U32, align_bytes=64)
+            w_scales = wq_pool.tile([P, N_TILE], U8, align_bytes=64)
+            nc.vector.quantize_mx(out=w_codes[:].bitcast(FP8X4), scales=w_scales[:], in_=w_grouped[:])
+            return w_codes, w_scales
+
+        def gate_by_channel(banks, j):
+            z_ps = banks.tile([P, TOKENS], F32, tag="bank")
+            nc.tensor.matmul(z_ps[:], lhsT=a2_sb[:, j * P : (j + 1) * P], rhs=hid_t[:], start=True, stop=True)
+            gate_t = gate_t_pool.tile([P, TOKENS], F32)
+            nc.scalar.activation(out=gate_t[:], in_=z_ps[:], func=ACT.Sigmoid, scale=-1.0, bias=neg[:, j : j + 1])
+            nc.gpsimd.tensor_scalar(
+                out=gate_t[:],
+                in0=gate_t[:],
+                scalar1=neg[:, CO // P + j : CO // P + j + 1],
+                scalar2=1.0,
+                op0=ALU.mult,
+                op1=ALU.add,
+            )
+            return gate_t
+
+        def gate_by_token(banks, n, b):
+            g_ps = banks.tile([P, N_TILE], F32, tag="bank")
+            for i in range(BLOCKS):
+                nc.tensor.transpose(
+                    g_ps[:, i * P : (i + 1) * P], gate_ts[n * BLOCKS + i][:, b * T : (b + 1) * T], ident_f32[:]
+                )
+            gate = gate_pool.tile([P, N_TILE], F32)
+            nc.scalar.copy(out=gate[:], in_=g_ps[:])
+            return gate
+
+        def multiply(sums, n, b):
+            k_ps = sums.tile([P, N_TILE], F32)
+            for g in range(PASSES):
+                w_codes, w_scales = quantised[n * PASSES + g]
+                nc.tensor.matmul_mx(
+                    out=k_ps[:],
+                    lhsT=xk_codes[:, g, b * T : (b + 1) * T].bitcast(FP8X4),
+                    lhsT_scale=xk_scales[:, g, b * T : (b + 1) * T],
+                    rhs=w_codes[:].bitcast(FP8X4),
+                    rhs_scale=w_scales[:],
+                    start=(g == 0),
+                    stop=(g == PASSES - 1),
+                )
+            return k_ps
+
+        def leave_psum(n, b, k_ps, gate):
+            cols = slice(n * N_TILE, (n + 1) * N_TILE)
+            scaled = tail.tile([P, N_TILE], F32, bufs=4)
+            nc.vector.tensor_tensor(out=scaled[:], in0=k_ps[:], in1=k_k_all[:, cols], op=ALU.mult)
+            k_out = tail.tile([P, N_TILE], F32)
+            nc.vector.tensor_tensor(out=k_out[:], in0=k_ps[:], in1=gate[:], op=ALU.mult)
+            nc.sync.dma_start(out=out_0[b, :, cols], in_=k_out[:])
+            squares = tail.tile([P, N_TILE], F32, bufs=2)
+            nc.scalar.activation(out=squares[:], in_=scaled[:], func=ACT.Square)
+            return n, b, scaled, squares
+
+        def normalise(n, b, scaled, squares):
+            sum_sq = tail.tile([P, HEADS], F32)
+            nc.vector.tensor_reduce(
+                out=sum_sq[:], in_=squares[:].rearrange("p (h d) -> p h d", d=HEAD), axis=mybir.AxisListType.X, op=ALU.add
+            )
+            nc.vector.tensor_scalar_max(out=sum_sq[:], in0=sum_sq[:], scalar1=NORM_FLOOR * NORM_FLOOR)
+            inv_sq = tail.tile([P, HEADS], F32)
+            nc.vector.reciprocal(out=inv_sq[:], in_=sum_sq[:])
+            inv_norm = tail.tile([P, HEADS], F32)
+            nc.scalar.sqrt(out=inv_norm[:], in_=inv_sq[:])
+            kk = tail.tile([P, N_TILE], F32)
+            nc.gpsimd.tensor_tensor(
+                out=kk[:].rearrange("p (h d) -> p h d", d=HEAD),
+                in0=scaled[:].rearrange("p (h d) -> p h d", d=HEAD),
+                in1=inv_norm[:].unsqueeze(2).to_broadcast([P, HEADS, HEAD]),
+                op=ALU.mult,
+            )
+            nc.sync.dma_start(out=out_1[b, :, n * N_TILE : (n + 1) * N_TILE], in_=kk[:])
+
+        gate_ts = []
+        quantised = []
+        gates = {}
+
+        with tc.psum_pool(name="early", bufs=BANKS) as early:
+            mix_ps = early.tile([P, 2, P], BF16, tag="bank")
+            for e in range(2):
+                nc.tensor.transpose(mix_ps[:, e, :], mix_rows[:, e:HALF:2], ident_bf[:])
+            nc.vector.tensor_copy(out=mix[:], in_=mix_ps[:, :, 0 : C // HALF])
+            nc.vector.tensor_scalar(
+                out=stay[:], in0=mix_ps[:, :, 0 : C // HALF], scalar1=-1.0, scalar2=1.0, op0=ALU.mult, op1=ALU.add
+            )
+            for g in range(PASSES):
+                planes = stage.tile([P, PACK, TOKENS], BF16)
+                for t in range(PACK):
+                    mix_channels(early, g, t, planes)
+                    if g > 0:
+                        gate_ts.append(gate_by_channel(early, len(gate_ts)))
+                if g == 0:
+                    neg_ps = early.tile([P, P], BF16, tag="bank")
+                    nc.tensor.transpose(neg_ps[:], gate_rows[:], ident_bf[:])
+                    nc.vector.tensor_scalar(
+                        out=neg[:], in0=neg_ps[:, 0 : 2 * CO // P], scalar1=-1.0, scalar2=None, op0=ALU.mult
+                    )
+                    hid_ps = early.tile([P, TOKENS], BF16, tag="bank")
+                    for b in range(SEQS):
+                        nc.tensor.transpose(hid_ps[:, b * T : (b + 1) * T], hid[:, b, :], ident_bf[:])
+                    nc.vector.tensor_copy(out=hid_t[:], in_=hid_ps[:])
+                quantise_tokens(g, planes)
+            for unit in range(PASSES + AHEAD):
+                quantised.append(quantise_weights(regroup_weights(early, unit)))
+                if len(gate_ts) < CO // P:
+                    gate_ts.append(gate_by_channel(early, len(gate_ts)))
+            for b in range(SEQS):
+                gates[(0, b)] = gate_by_token(early, 0, b)
+
+        with tc.psum_pool(name="work", bufs=BANKS - SEQS, reuse_waits="tile") as work, tc.psum_pool(
+            name="sums", bufs=SEQS, reuse_waits="tile"
+        ) as sums:
+            waiting = None
+            for step in range(N_TILES * SEQS):
+                n, b = divmod(step, SEQS)
+                k_ps = multiply(sums, n, b)
+                unit = len(quantised)
+                if unit < UNITS:
+                    w_grouped = regroup_weights(work, unit)
+                if n + 1 < N_TILES:
+                    gates[(n + 1, b)] = gate_by_token(work, n + 1, b)
+                left = leave_psum(n, b, k_ps, gates[(n, b)])
+                if waiting is not None:
+                    normalise(*waiting)
+                waiting = left
+                if unit < UNITS:
+                    quantised.append(quantise_weights(w_grouped))
+            normalise(*waiting)

@@ -49,6 +49,10 @@ def tile_full_tmix_params_pa_kernel(tc, x, x_k, W_k, a_hid, a2, a0, k_k, k_a, ou
         gate_pool = ctx.enter_context(tc.tile_pool(name="gate_pool", bufs=SEQS + 2))
         tail = ctx.enter_context(tc.tile_pool(name="tail", bufs=3))
 
+        warm = keep.tile([P, 2], F32)
+        nc.vector.memset(warm[:], 0.0)
+        nc.scalar.activation(out=warm[:, 1:2], in_=warm[:, 0:1], func=ACT.Sigmoid)
+
         ident_bf = keep.tile([P, P], BF16)
         make_identity(nc, ident_bf[:])
         ident_f32 = keep.tile([P, P], F32)
@@ -117,12 +121,15 @@ def tile_full_tmix_params_pa_kernel(tc, x, x_k, W_k, a_hid, a2, a0, k_k, k_a, ou
                 op1=ALU.add,
             )
 
-        def quantise_tokens(g, planes):
+        def regroup_tokens(planes):
             grouped = stage.tile([P, TOKENS * PACK], BF16, align_bytes=64)
             nc.vector.tensor_copy(
                 out=grouped[:].rearrange("p (c i t) -> p c t i", i=4, t=PACK),
                 in_=planes[:].rearrange("p t (c i) -> p c t i", i=4),
             )
+            return grouped
+
+        def quantise_tokens(g, grouped):
             nc.vector.quantize_mx(out=xk_codes[:, g, :].bitcast(FP8X4), scales=xk_scales[:, g, :], in_=grouped[:])
 
         def regroup_weights(banks, unit):
@@ -191,23 +198,31 @@ def tile_full_tmix_params_pa_kernel(tc, x, x_k, W_k, a_hid, a2, a0, k_k, k_a, ou
                 )
             return k_ps
 
-        def leave_psum(n, b, k_ps, gate):
-            cols = slice(n * N_TILE, (n + 1) * N_TILE)
+        def scale_by_k_k(n, k_ps):
             scaled = tail.tile([P, N_TILE], F32, bufs=4)
-            nc.vector.tensor_tensor(out=scaled[:], in0=k_ps[:], in1=k_k_all[:, cols], op=ALU.mult)
-            k_out = tail.tile([P, N_TILE], F32)
-            nc.vector.tensor_tensor(out=k_out[:], in0=k_ps[:], in1=gate[:], op=ALU.mult)
-            nc.sync.dma_start(out=out_0[b, :, cols], in_=k_out[:])
+            nc.vector.tensor_tensor(
+                out=scaled[:], in0=k_ps[:], in1=k_k_all[:, n * N_TILE : (n + 1) * N_TILE], op=ALU.mult
+            )
             squares = tail.tile([P, N_TILE], F32, bufs=2)
             nc.scalar.activation(out=squares[:], in_=scaled[:], func=ACT.Square)
-            return n, b, scaled, squares
+            return scaled, squares
 
-        def normalise(n, b, scaled, squares):
+        def store_k_out(n, b, k_ps, gate):
+            k_out = tail.tile([P, N_TILE], F32)
+            nc.vector.tensor_tensor(out=k_out[:], in0=k_ps[:], in1=gate[:], op=ALU.mult)
+            nc.sync.dma_start(out=out_0[b, :, n * N_TILE : (n + 1) * N_TILE], in_=k_out[:])
+
+        def sum_squares(squares):
             sum_sq = tail.tile([P, HEADS], F32)
             nc.vector.tensor_reduce(
                 out=sum_sq[:], in_=squares[:].rearrange("p (h d) -> p h d", d=HEAD), axis=mybir.AxisListType.X, op=ALU.add
             )
+            return sum_sq
+
+        def floor_sums(sum_sq):
             nc.vector.tensor_scalar_max(out=sum_sq[:], in0=sum_sq[:], scalar1=NORM_FLOOR * NORM_FLOOR)
+
+        def store_kk(n, b, scaled, sum_sq):
             inv_sq = tail.tile([P, HEADS], F32)
             nc.vector.reciprocal(out=inv_sq[:], in_=sum_sq[:])
             inv_norm = tail.tile([P, HEADS], F32)
@@ -234,11 +249,16 @@ def tile_full_tmix_params_pa_kernel(tc, x, x_k, W_k, a_hid, a2, a0, k_k, k_a, ou
                 out=stay[:], in0=mix_ps[:, :, 0 : C // HALF], scalar1=-1.0, scalar2=1.0, op0=ALU.mult, op1=ALU.add
             )
             for g in range(PASSES):
+                mixed = planes if g > 0 else None
                 planes = stage.tile([P, PACK, TOKENS], BF16)
                 for t in range(PACK):
                     mix_channels(early, g, t, planes)
                     if g > 0:
                         gate_ts.append(gate_by_channel(early, len(gate_ts)))
+                    if g > 0 and t == 0:
+                        grouped = regroup_tokens(mixed)
+                    if g > 0 and t == 1:
+                        quantise_tokens(g - 1, grouped)
                 if g == 0:
                     neg_ps = early.tile([P, P], BF16, tag="bank")
                     nc.tensor.transpose(neg_ps[:], gate_rows[:], ident_bf[:])
@@ -249,7 +269,7 @@ def tile_full_tmix_params_pa_kernel(tc, x, x_k, W_k, a_hid, a2, a0, k_k, k_a, ou
                     for b in range(SEQS):
                         nc.tensor.transpose(hid_ps[:, b * T : (b + 1) * T], hid[:, b, :], ident_bf[:])
                     nc.vector.tensor_copy(out=hid_t[:], in_=hid_ps[:])
-                quantise_tokens(g, planes)
+            quantise_tokens(PASSES - 1, regroup_tokens(planes))
             for unit in range(PASSES + AHEAD):
                 quantised.append(quantise_weights(regroup_weights(early, unit)))
                 if len(gate_ts) < CO // P:
@@ -260,7 +280,7 @@ def tile_full_tmix_params_pa_kernel(tc, x, x_k, W_k, a_hid, a2, a0, k_k, k_a, ou
         with tc.psum_pool(name="work", bufs=BANKS - SEQS, reuse_waits="tile") as work, tc.psum_pool(
             name="sums", bufs=SEQS, reuse_waits="tile"
         ) as sums:
-            waiting = None
+            before = None
             for step in range(N_TILES * SEQS):
                 n, b = divmod(step, SEQS)
                 k_ps = multiply(sums, n, b)
@@ -269,10 +289,17 @@ def tile_full_tmix_params_pa_kernel(tc, x, x_k, W_k, a_hid, a2, a0, k_k, k_a, ou
                     w_grouped = regroup_weights(work, unit)
                 if n + 1 < N_TILES:
                     gates[(n + 1, b)] = gate_by_token(work, n + 1, b)
-                left = leave_psum(n, b, k_ps, gates[(n, b)])
-                if waiting is not None:
-                    normalise(*waiting)
-                waiting = left
+                if before is not None:
+                    sum_sq = sum_squares(before[3])
+                scaled, squares = scale_by_k_k(n, k_ps)
+                if before is not None:
+                    floor_sums(sum_sq)
+                store_k_out(n, b, k_ps, gates[(n, b)])
+                if before is not None:
+                    store_kk(before[0], before[1], before[2], sum_sq)
                 if unit < UNITS:
                     quantised.append(quantise_weights(w_grouped))
-            normalise(*waiting)
+                before = (n, b, scaled, squares)
+            sum_sq = sum_squares(before[3])
+            floor_sums(sum_sq)
+            store_kk(before[0], before[1], before[2], sum_sq)

@@ -31,6 +31,8 @@ BANK_WORDS = 512
 BANKS = 8
 UNITS = N_TILES * PASSES
 AHEAD = 1
+STEPS = N_TILES * SEQS
+RUN = 2
 NORM_FLOOR = 1e-12
 
 FLOPS = 2 * TOKENS * C * CO + 2 * TOKENS * DA * CO
@@ -46,7 +48,7 @@ def tile_full_tmix_params_pa_kernel(tc, x, x_k, W_k, a_hid, a2, a0, k_k, k_a, ou
         stage = ctx.enter_context(tc.tile_pool(name="stage", bufs=2))
         wq_pool = ctx.enter_context(tc.tile_pool(name="wq_pool", bufs=2 * PASSES + AHEAD))
         gate_t_pool = ctx.enter_context(tc.tile_pool(name="gate_t_pool", bufs=CO // P))
-        gate_pool = ctx.enter_context(tc.tile_pool(name="gate_pool", bufs=SEQS + 2))
+        gate_pool = ctx.enter_context(tc.tile_pool(name="gate_pool", bufs=3))
         tail = ctx.enter_context(tc.tile_pool(name="tail", bufs=3))
 
         warm = keep.tile([P, 2], F32)
@@ -222,13 +224,13 @@ def tile_full_tmix_params_pa_kernel(tc, x, x_k, W_k, a_hid, a2, a0, k_k, k_a, ou
         def floor_sums(sum_sq):
             nc.vector.tensor_scalar_max(out=sum_sq[:], in0=sum_sq[:], scalar1=NORM_FLOOR * NORM_FLOOR)
 
-        def store_kk(n, b, scaled, sum_sq):
+        def store_kk(n, b, scaled, sum_sq, multiplier):
             inv_sq = tail.tile([P, HEADS], F32)
             nc.vector.reciprocal(out=inv_sq[:], in_=sum_sq[:])
             inv_norm = tail.tile([P, HEADS], F32)
             nc.scalar.sqrt(out=inv_norm[:], in_=inv_sq[:])
             kk = tail.tile([P, N_TILE], F32)
-            nc.gpsimd.tensor_tensor(
+            multiplier.tensor_tensor(
                 out=kk[:].rearrange("p (h d) -> p h d", d=HEAD),
                 in0=scaled[:].rearrange("p (h d) -> p h d", d=HEAD),
                 in1=inv_norm[:].unsqueeze(2).to_broadcast([P, HEADS, HEAD]),
@@ -274,32 +276,33 @@ def tile_full_tmix_params_pa_kernel(tc, x, x_k, W_k, a_hid, a2, a0, k_k, k_a, ou
                 quantised.append(quantise_weights(regroup_weights(early, unit)))
                 if len(gate_ts) < CO // P:
                     gate_ts.append(gate_by_channel(early, len(gate_ts)))
-            for b in range(SEQS):
-                gates[(0, b)] = gate_by_token(early, 0, b)
+            gates[0] = gate_by_token(early, 0, 0)
 
         with tc.psum_pool(name="work", bufs=BANKS - SEQS, reuse_waits="tile") as work, tc.psum_pool(
             name="sums", bufs=SEQS, reuse_waits="tile"
         ) as sums:
             before = None
-            for step in range(N_TILES * SEQS):
-                n, b = divmod(step, SEQS)
-                k_ps = multiply(sums, n, b)
-                unit = len(quantised)
-                if unit < UNITS:
-                    w_grouped = regroup_weights(work, unit)
-                if n + 1 < N_TILES:
-                    gates[(n + 1, b)] = gate_by_token(work, n + 1, b)
-                if before is not None:
-                    sum_sq = sum_squares(before[3])
-                scaled, squares = scale_by_k_k(n, k_ps)
-                if before is not None:
-                    floor_sums(sum_sq)
-                store_k_out(n, b, k_ps, gates[(n, b)])
-                if before is not None:
-                    store_kk(before[0], before[1], before[2], sum_sq)
-                if unit < UNITS:
-                    quantised.append(quantise_weights(w_grouped))
-                before = (n, b, scaled, squares)
+            for first in range(0, STEPS, RUN):
+                products = [multiply(sums, *divmod(step, SEQS)) for step in range(first, first + RUN)]
+                for step in range(first, first + RUN):
+                    n, b = divmod(step, SEQS)
+                    k_ps = products[step - first]
+                    unit = len(quantised)
+                    if unit < UNITS:
+                        w_grouped = regroup_weights(work, unit)
+                    if step + 1 < STEPS:
+                        gates[step + 1] = gate_by_token(work, *divmod(step + 1, SEQS))
+                    if before is not None:
+                        sum_sq = sum_squares(before[3])
+                    scaled, squares = scale_by_k_k(n, k_ps)
+                    if before is not None:
+                        floor_sums(sum_sq)
+                    store_k_out(n, b, k_ps, gates[step])
+                    if before is not None:
+                        store_kk(before[0], before[1], before[2], sum_sq, nc.gpsimd)
+                    if unit < UNITS:
+                        quantised.append(quantise_weights(w_grouped))
+                    before = (n, b, scaled, squares)
             sum_sq = sum_squares(before[3])
             floor_sums(sum_sq)
-            store_kk(before[0], before[1], before[2], sum_sq)
+            store_kk(before[0], before[1], before[2], sum_sq, nc.vector)

@@ -32,7 +32,6 @@ BANKS = 8
 UNITS = N_TILES * PASSES
 AHEAD = 1
 STEPS = N_TILES * SEQS
-RUN = 2
 NORM_FLOOR = 1e-12
 
 FLOPS = 2 * TOKENS * C * CO + 2 * TOKENS * DA * CO
@@ -282,27 +281,25 @@ def tile_full_tmix_params_pa_kernel(tc, x, x_k, W_k, a_hid, a2, a0, k_k, k_a, ou
             name="sums", bufs=SEQS, reuse_waits="tile"
         ) as sums:
             before = None
-            for first in range(0, STEPS, RUN):
-                products = [multiply(sums, *divmod(step, SEQS)) for step in range(first, first + RUN)]
-                for step in range(first, first + RUN):
-                    n, b = divmod(step, SEQS)
-                    k_ps = products[step - first]
-                    unit = len(quantised)
-                    if unit < UNITS:
-                        w_grouped = regroup_weights(work, unit)
-                    if step + 1 < STEPS:
-                        gates[step + 1] = gate_by_token(work, *divmod(step + 1, SEQS))
-                    if before is not None:
-                        sum_sq = sum_squares(before[3])
-                    scaled, squares = scale_by_k_k(n, k_ps)
-                    if before is not None:
-                        floor_sums(sum_sq)
-                    store_k_out(n, b, k_ps, gates[step])
-                    if before is not None:
-                        store_kk(before[0], before[1], before[2], sum_sq, nc.gpsimd)
-                    if unit < UNITS:
-                        quantised.append(quantise_weights(w_grouped))
-                    before = (n, b, scaled, squares)
+            for step in range(STEPS):
+                n, b = divmod(step, SEQS)
+                k_ps = multiply(sums, n, b)
+                unit = len(quantised)
+                if unit < UNITS:
+                    w_grouped = regroup_weights(work, unit)
+                if step + 1 < STEPS:
+                    gates[step + 1] = gate_by_token(work, *divmod(step + 1, SEQS))
+                if before is not None:
+                    sum_sq = sum_squares(before[3])
+                scaled, squares = scale_by_k_k(n, k_ps)
+                if before is not None:
+                    floor_sums(sum_sq)
+                store_k_out(n, b, k_ps, gates[step])
+                if before is not None:
+                    store_kk(before[0], before[1], before[2], sum_sq, nc.gpsimd)
+                if unit < UNITS:
+                    quantised.append(quantise_weights(w_grouped))
+                before = (n, b, scaled, squares)
             sum_sq = sum_squares(before[3])
             floor_sums(sum_sq)
             store_kk(before[0], before[1], before[2], sum_sq, nc.vector)

from contextlib import ExitStack

import concourse.mybir as mybir
from concourse.masks import make_identity

BF16 = mybir.dt.bfloat16
F32 = mybir.dt.float32
U32 = mybir.dt.uint32
U8 = mybir.dt.uint8
FP8X4 = mybir.dt.float8_e4m3fn_x4
ACT = mybir.ActivationFunctionType
ALU = mybir.AluOpType

P = 128
SEQS = 4
T = 128
TOKENS = SEQS * T
C = 2048
CO = 2048
DA = 128
HEAD = 64
PACK = 4
K_PASS = P * PACK
PASSES = C // K_PASS
HALF = K_PASS // 2
N_TILE = 512
N_TILES = CO // N_TILE
BLOCKS = N_TILE // P
HEADS = N_TILE // HEAD
BANK_WORDS = 512
BANKS = 8
UNITS = N_TILES * PASSES
AHEAD = 1
STEPS = N_TILES * SEQS
NORM_FLOOR = 1e-12

FLOPS = 2 * TOKENS * C * CO + 2 * TOKENS * DA * CO


def tile_full_tmix_params_pa_kernel(tc, x, x_k, W_k, a_hid, a2, a0, k_k, k_a, out_0, out_1):
    nc = tc.nc
    with ExitStack() as ctx:
        ctx.enter_context(tc.manual_schedule())
        keep = ctx.enter_context(tc.tile_pool(name="keep", bufs=1))
        x_pool = ctx.enter_context(tc.tile_pool(name="x_pool", bufs=PASSES))
        w_pool = ctx.enter_context(tc.tile_pool(name="w_pool", bufs=CO // P))
        stage = ctx.enter_context(tc.tile_pool(name="stage", bufs=2))
        wq_pool = ctx.enter_context(tc.tile_pool(name="wq_pool", bufs=2 * PASSES + AHEAD))
        gate_t_pool = ctx.enter_context(tc.tile_pool(name="gate_t_pool", bufs=CO // P))
        gate_pool = ctx.enter_context(tc.tile_pool(name="gate_pool", bufs=3))
        tail = ctx.enter_context(tc.tile_pool(name="tail", bufs=3))

        warm = keep.tile([P, 2], F32)
        nc.vector.memset(warm[:], 0.0)
        nc.scalar.activation(out=warm[:, 1:2], in_=warm[:, 0:1], func=ACT.Sigmoid)

        ident_bf = keep.tile([P, P], BF16)
        make_identity(nc, ident_bf[:])
        ident_f32 = keep.tile([P, P], F32)
        make_identity(nc, ident_f32[:])

        mix_rows = keep.tile([P, HALF], BF16)
        nc.vector.memset(mix_rows[:], 0.0)
        gate_rows = keep.tile([P, P], BF16)
        nc.vector.memset(gate_rows[:], 0.0)
        hid = keep.tile([P, SEQS, DA], BF16)
        a2_sb = keep.tile([DA, CO], BF16)
        k_k_all = keep.tile([P, CO], BF16)

        nc.sync.dma_start(out=mix_rows[0 : C // HALF, :], in_=x_k.rearrange("a b (r c) -> (a b r) c", c=HALF))
        x_tiles = []
        for g in range(PASSES):
            x_g = x_pool.tile([P, SEQS, K_PASS], BF16, name="x_g")
            nc.sync.dma_start(out=x_g[:], in_=x[:, :, g * K_PASS : (g + 1) * K_PASS].rearrange("b t c -> t b c"))
            x_tiles.append(x_g)
            if g == 0:
                nc.sync.dma_start(out=hid[:], in_=a_hid.rearrange("b t d -> t b d"))
                nc.sync.dma_start(out=a2_sb[:], in_=a2)
                nc.sync.dma_start(out=gate_rows[0 : CO // P, :], in_=a0.rearrange("a b (j p) -> (a b j) p", p=P))
                nc.sync.dma_start(
                    out=gate_rows[CO // P : 2 * CO // P, :], in_=k_a.rearrange("a b (j p) -> (a b j) p", p=P)
                )
        w_tiles = []
        for i in range(CO // P):
            w_i = w_pool.tile([P, C], BF16, name="w_i")
            nc.sync.dma_start(out=w_i[:], in_=W_k[i * P : (i + 1) * P, :])
            w_tiles.append(w_i)
            if i == BLOCKS - 1:
                nc.sync.dma_start(out=k_k_all[:], in_=k_k.rearrange("a b c -> (a b c)").partition_broadcast(P))

        mix = keep.tile([P, 2, C // HALF], F32)
        stay = keep.tile([P, 2, C // HALF], F32)
        neg = keep.tile([P, 2 * CO // P], F32)
        hid_t = keep.tile([DA, TOKENS], BF16)
        xk_codes = keep.tile([P, PASSES, TOKENS], U32, align_bytes=64)
        xk_scales = keep.tile([P, PASSES, TOKENS], U8, align_bytes=64)
        shifted_ring = [keep.tile([P, SEQS, T], F32, name="shifted%d" % i) for i in range(3)]
        for shifted in shifted_ring:
            nc.vector.memset(shifted[:, :, 0:1], 0.0)

        def mix_channels(banks, g, t, planes):
            u, e = divmod(t, 2)
            r = 2 * g + u
            x_t = banks.tile([P, TOKENS], BF16, tag="bank")
            for b in range(SEQS):
                nc.tensor.transpose(
                    x_t[:, b * T : (b + 1) * T], x_tiles[g][:, b, u * HALF + e : (u + 1) * HALF : 2], ident_bf[:]
                )
            shifted = shifted_ring[(g * PACK + t) % len(shifted_ring)]
            nc.scalar.activation(
                out=shifted[:, :, 1:T],
                in_=x_t[:].rearrange("p (b r) -> p b r", b=SEQS)[:, :, 0 : T - 1],
                func=ACT.Copy,
                scale=mix[:, e, r : r + 1],
            )
            nc.vector.scalar_tensor_tensor(
                out=planes[:, t, :],
                in0=x_t[:],
                scalar=stay[:, e, r : r + 1],
                in1=shifted[:].rearrange("p b r -> p (b r)"),
                op0=ALU.mult,
                op1=ALU.add,
            )

        def regroup_tokens(planes):
            grouped = stage.tile([P, TOKENS * PACK], BF16, align_bytes=64)
            nc.vector.tensor_copy(
                out=grouped[:].rearrange("p (c i t) -> p c t i", i=4, t=PACK),
                in_=planes[:].rearrange("p t (c i) -> p c t i", i=4),
            )
            return grouped

        def quantise_tokens(g, grouped):
            nc.vector.quantize_mx(out=xk_codes[:, g, :].bitcast(FP8X4), scales=xk_scales[:, g, :], in_=grouped[:])

        def regroup_weights(banks, unit):
            n, g = divmod(unit, PASSES)
            w_grouped = stage.tile([P, N_TILE * PACK], BF16, align_bytes=64, bufs=3)
            words = w_grouped[:].bitcast(F32)
            for h in range(BLOCKS // 2):
                w_t = banks.tile([P, 2, 2 * P], F32, tag="bank")
                for u in range(2):
                    for i in range(2):
                        first = (g * K_PASS + u * HALF) // 2
                        nc.tensor.transpose(
                            w_t[:, u, i * P : (i + 1) * P],
                            w_tiles[n * BLOCKS + 2 * h + i][:].bitcast(F32)[:, first : first + P],
                            ident_f32[:],
                        )
                nc.scalar.copy(
                    out=words[:, h * BANK_WORDS : (h + 1) * BANK_WORDS].rearrange("p (c u) -> p c u", u=2),
                    in_=w_t[:].rearrange("p u c -> p c u"),
                )
            return w_grouped

        def quantise_weights(w_grouped):
            w_codes = wq_pool.tile([P, N_TILE], U32, align_bytes=64)
            w_scales = wq_pool.tile([P, N_TILE], U8, align_bytes=64)
            nc.vector.quantize_mx(out=w_codes[:].bitcast(FP8X4), scales=w_scales[:], in_=w_grouped[:])
            return w_codes, w_scales

        def gate_by_channel(banks, j):
            z_ps = banks.tile([P, TOKENS], F32, tag="bank")
            nc.tensor.matmul(z_ps[:], lhsT=a2_sb[:, j * P : (j + 1) * P], rhs=hid_t[:], start=True, stop=True)
            gate_t = gate_t_pool.tile([P, TOKENS], F32)
            nc.scalar.activation(out=gate_t[:], in_=z_ps[:], func=ACT.Sigmoid, scale=-1.0, bias=neg[:, j : j + 1])
            nc.gpsimd.tensor_scalar(
                out=gate_t[:],
                in0=gate_t[:],
                scalar1=neg[:, CO // P + j : CO // P + j + 1],
                scalar2=1.0,
                op0=ALU.mult,
                op1=ALU.add,
            )
            return gate_t

        def gate_by_token(banks, n, b):
            g_ps = banks.tile([P, N_TILE], F32, tag="bank")
            for i in range(BLOCKS):
                nc.tensor.transpose(
                    g_ps[:, i * P : (i + 1) * P], gate_ts[n * BLOCKS + i][:, b * T : (b + 1) * T], ident_f32[:]
                )
            gate = gate_pool.tile([P, N_TILE], F32)
            nc.scalar.copy(out=gate[:], in_=g_ps[:])
            return gate

        def multiply(sums, n, b):
            k_ps = sums.tile([P, N_TILE], F32)
            for g in range(PASSES):
                w_codes, w_scales = quantised[n * PASSES + g]
                nc.tensor.matmul_mx(
                    out=k_ps[:],
                    lhsT=xk_codes[:, g, b * T : (b + 1) * T].bitcast(FP8X4),
                    lhsT_scale=xk_scales[:, g, b * T : (b + 1) * T],
                    rhs=w_codes[:].bitcast(FP8X4),
                    rhs_scale=w_scales[:],
                    start=(g == 0),
                    stop=(g == PASSES - 1),
                )
            return k_ps

        def scale_by_k_k(n, k_ps):
            scaled = tail.tile([P, N_TILE], F32, bufs=4)
            nc.vector.tensor_tensor(
                out=scaled[:], in0=k_ps[:], in1=k_k_all[:, n * N_TILE : (n + 1) * N_TILE], op=ALU.mult
            )
            squares = tail.tile([P, N_TILE], F32, bufs=2)
            nc.scalar.activation(out=squares[:], in_=scaled[:], func=ACT.Square)
            return scaled, squares

        def store_k_out(n, b, k_ps, gate):
            k_out = tail.tile([P, N_TILE], F32)
            nc.vector.tensor_tensor(out=k_out[:], in0=k_ps[:], in1=gate[:], op=ALU.mult)
            nc.sync.dma_start(out=out_0[b, :, n * N_TILE : (n + 1) * N_TILE], in_=k_out[:])

        def sum_squares(squares):
            sum_sq = tail.tile([P, HEADS], F32)
            nc.vector.tensor_reduce(
                out=sum_sq[:], in_=squares[:].rearrange("p (h d) -> p h d", d=HEAD), axis=mybir.AxisListType.X, op=ALU.add
            )
            return sum_sq

        def floor_sums(sum_sq):
            nc.vector.tensor_scalar_max(out=sum_sq[:], in0=sum_sq[:], scalar1=NORM_FLOOR * NORM_FLOOR)

        def store_kk(n, b, scaled, sum_sq, multiplier):
            inv_sq = tail.tile([P, HEADS], F32)
            nc.vector.reciprocal(out=inv_sq[:], in_=sum_sq[:])
            inv_norm = tail.tile([P, HEADS], F32)
            nc.scalar.sqrt(out=inv_norm[:], in_=inv_sq[:])
            kk = tail.tile([P, N_TILE], F32)
            multiplier.tensor_tensor(
                out=kk[:].rearrange("p (h d) -> p h d", d=HEAD),
                in0=scaled[:].rearrange("p (h d) -> p h d", d=HEAD),
                in1=inv_norm[:].unsqueeze(2).to_broadcast([P, HEADS, HEAD]),
                op=ALU.mult,
            )
            nc.sync.dma_start(out=out_1[b, :, n * N_TILE : (n + 1) * N_TILE], in_=kk[:])

        gate_ts = []
        quantised = []
        gates = {}

        with tc.psum_pool(name="early", bufs=BANKS) as early:
            mix_ps = early.tile([P, 2, P], BF16, tag="bank")
            for e in range(2):
                nc.tensor.transpose(mix_ps[:, e, :], mix_rows[:, e:HALF:2], ident_bf[:])
            nc.vector.tensor_copy(out=mix[:], in_=mix_ps[:, :, 0 : C // HALF])
            nc.vector.tensor_scalar(
                out=stay[:], in0=mix_ps[:, :, 0 : C // HALF], scalar1=-1.0, scalar2=1.0, op0=ALU.mult, op1=ALU.add
            )
            for g in range(PASSES):
                mixed = planes if g > 0 else None
                planes = stage.tile([P, PACK, TOKENS], BF16)
                for t in range(PACK):
                    mix_channels(early, g, t, planes)
                    if g > 0:
                        gate_ts.append(gate_by_channel(early, len(gate_ts)))
                    if g > 0 and t == 0:
                        grouped = regroup_tokens(mixed)
                    if g > 0 and t == 1:
                        quantise_tokens(g - 1, grouped)
                if g == 0:
                    neg_ps = early.tile([P, P], BF16, tag="bank")
                    nc.tensor.transpose(neg_ps[:], gate_rows[:], ident_bf[:])
                    nc.vector.tensor_scalar(
                        out=neg[:], in0=neg_ps[:, 0 : 2 * CO // P], scalar1=-1.0, scalar2=None, op0=ALU.mult
                    )
                    hid_ps = early.tile([P, TOKENS], BF16, tag="bank")
                    for b in range(SEQS):
                        nc.tensor.transpose(hid_ps[:, b * T : (b + 1) * T], hid[:, b, :], ident_bf[:])
                    nc.vector.tensor_copy(out=hid_t[:], in_=hid_ps[:])
            quantise_tokens(PASSES - 1, regroup_tokens(planes))
            for unit in range(PASSES + AHEAD):
                quantised.append(quantise_weights(regroup_weights(early, unit)))
                if len(gate_ts) < CO // P:
                    gate_ts.append(gate_by_channel(early, len(gate_ts)))
            gates[0] = gate_by_token(early, 0, 0)

        with tc.psum_pool(name="work", bufs=BANKS - SEQS, reuse_waits="tile") as work, tc.psum_pool(
            name="sums", bufs=SEQS, reuse_waits="tile"
        ) as sums:
            before = None
            for step in range(STEPS):
                n, b = divmod(step, SEQS)
                k_ps = multiply(sums, n, b)
                unit = len(quantised)
                if unit < UNITS:
                    w_grouped = regroup_weights(work, unit)
                if step + 1 < STEPS:
                    gates[step + 1] = gate_by_token(work, *divmod(step + 1, SEQS))
                if before is not None:
                    sum_sq = sum_squares(before[3])
                scaled, squares = scale_by_k_k(n, k_ps)
                if before is not None:
                    floor_sums(sum_sq)
                store_k_out(n, b, k_ps, gates[step])
                if before is not None:
                    store_kk(before[0], before[1], before[2], sum_sq, nc.gpsimd)
                if unit < UNITS:
                    quantised.append(quantise_weights(w_grouped))
                before = (n, b, scaled, squares)
            sum_sq = sum_squares(before[3])
            floor_sums(sum_sq)
            store_kk(before[0], before[1], before[2], sum_sq, nc.vector)
